import numpy as np
import ml_dtypes


def mxq(x, axis, fmt="e4m3"):
    dtype, down = {"e4m3": (ml_dtypes.float8_e4m3fn, 7), "e5m2": (ml_dtypes.float8_e5m2, 14)}[fmt]
    v = np.moveaxis(np.asarray(x, np.float32).astype(ml_dtypes.bfloat16).astype(np.float64), axis, -1)
    blocks = v.reshape(v.shape[:-1] + (-1, 32))
    amax = np.abs(blocks).max(-1, keepdims=True)
    byte = np.maximum(np.where(amax > 0, np.frexp(amax)[1] - 1 + 127, 0) - down, 1)
    scale = np.exp2(byte - 127.0)
    codes = (blocks / scale).astype(np.float32).astype(dtype).astype(np.float64)
    return np.moveaxis((codes * scale).reshape(v.shape), -1, axis)


WIDE = False


def mx_kscale(k):
    if not WIDE:
        return np.ones(k)
    levels = np.array([10, -10, 5, -5, 0])
    a = np.random.permutation(np.resize(levels, k // 512 * 4)).reshape(k // 512, 4)
    idx = np.arange(k)
    return np.exp2(a[idx // 512, idx % 128 // 32])


BF16 = ml_dtypes.bfloat16


def bf(x):
    return np.asarray(x, np.float32).astype(BF16)


def f64(x):
    return np.asarray(x).astype(np.float64)


B, T, KA, KT, DIM, NH, HD, E = 16, 512, 256, 256, 512, 1, 128, 8
ROPE_BASE = 10000.0


def rope_cos_sin(L, hd):
    inv_freq = 1.0 / (ROPE_BASE ** (f64(np.arange(0, hd, 2)) / hd))
    freqs = f64(np.arange(L))[:, None] * inv_freq[None, :]
    emb = np.concatenate([freqs, freqs], axis=-1)
    return np.cos(emb), np.sin(emb)


def rotate_half(x):
    x1 = x[..., 0::2]
    x2 = x[..., 1::2]
    return np.stack((-x2, x1), axis=-1).reshape(x.shape)


def rope(t, cos, sin):
    return t * cos[None, None] + rotate_half(t) * sin[None, None]


def heads(t):
    return t.reshape(B, -1, NH, HD).transpose(0, 2, 1, 3)


def setup_inputs():
    s = mx_kscale(DIM)
    c = 1.2 / np.sqrt(DIM)
    return {"x": bf(np.random.standard_normal((B, T, DIM)) * s),
            "W_qa": bf(np.random.standard_normal((NH * HD, DIM)) * c / s[None, :]),
            "b_qa": bf(np.random.standard_normal(NH * HD) * 0.3),
            "W_qt": bf(np.random.standard_normal((NH * HD, DIM)) * c / s[None, :]),
            "b_qt": bf(np.random.standard_normal(NH * HD) * 0.3)}


def reference(x, W_qa, b_qa, W_qt, b_qt):
    xq = mxq(f64(x), 2, "e4m3")
    q_a = heads((xq @ mxq(f64(W_qa), 1, "e4m3").T) + f64(b_qa))
    q_t = heads((xq @ mxq(f64(W_qt), 1, "e4m3").T) + f64(b_qt))
    cos_m, sin_m = rope_cos_sin(T, HD)
    return rope(q_a, cos_m, sin_m), rope(q_t, cos_m, sin_m)

@@ -1,0 +1,212 @@
+import math
+from contextlib import ExitStack
+
+import concourse.mybir as mybir
+from concourse.masks import make_identity
+
+F32 = mybir.dt.float32
+BF16 = mybir.dt.bfloat16
+I32 = mybir.dt.int32
+U32 = mybir.dt.uint32
+U8 = mybir.dt.uint8
+FP8X4 = mybir.dt.float8_e4m3fn_x4
+ALU = mybir.AluOpType
+ACT = mybir.ActivationFunctionType
+
+P = 128
+NB = 16
+T = 512
+K = 512
+D = 128
+TI = 4
+
+FLOPS = 2 * NB * T * K * 2 * D
+
+
+def tile_l1regressionmoeactionhead_pa_t_kernel(tc, x, W_qa, b_qa, W_qt, b_qt, out_0, out_1):
+    nc = tc.nc
+    outs = (out_0, out_1)
+    with ExitStack() as ctx:
+        const = ctx.enter_context(tc.tile_pool(name="const", bufs=1))
+        xin = ctx.enter_context(tc.tile_pool(name="xin", bufs=NB))
+        grp = ctx.enter_context(tc.tile_pool(name="grp", bufs=3))
+        cod = ctx.enter_context(tc.tile_pool(name="cod", bufs=3))
+        prod = ctx.enter_context(tc.tile_pool(name="prod", bufs=4))
+        ost = ctx.enter_context(tc.tile_pool(name="ost", bufs=4))
+        psx = ctx.enter_context(tc.psum_pool(name="psx", bufs=2))
+        psp = ctx.enter_context(tc.psum_pool(name="psp", bufs=4))
+        pso = ctx.enter_context(tc.psum_pool(name="pso", bufs=2))
+
+        w_sb = []
+        for w, W in enumerate((W_qa, W_qt)):
+            wt = const.tile([P, K], BF16, name="w_sb%d" % w)
+            nc.scalar.dma_start(out=wt[:], in_=W)
+            w_sb.append(wt)
+        brow = const.tile([P, D], BF16, name="brow")
+        nc.vector.memset(brow[:], 0.0)
+        nc.scalar.dma_start(out=brow[0:1, :], in_=b_qa.unsqueeze(0))
+        nc.scalar.dma_start(out=brow[1:2, :], in_=b_qt.unsqueeze(0))
+        x_sb = []
+        for n in range(NB):
+            xt_in = xin.tile([P, TI * K], BF16, name="x_sb")
+            nc.sync.dma_start(out=xt_in[:], in_=x[n].rearrange("(p i) k -> p (i k)", i=TI))
+            x_sb.append(xt_in)
+
+        ident = const.tile([P, P], F32, name="ident")
+        make_identity(nc, ident[:])
+        perm = const.tile([P, P], F32, name="perm")
+        ident_v = ident[:].rearrange("p (i e) -> p i e", e=2)
+        perm_v = perm[:].rearrange("p (i e) -> p i e", e=2)
+        nc.vector.tensor_copy(out=perm_v[:, :, 0], in_=ident_v[:, :, 1])
+        nc.vector.tensor_copy(out=perm_v[:, :, 1], in_=ident_v[:, :, 0])
+
+        ti = const.tile([P, T], I32, name="ti")
+        nc.gpsimd.iota(ti[:], pattern=[[1, TI], [TI, P]], base=0, channel_multiplier=0)
+
+        ratio = 10000.0 ** (-1.0 / 64.0)
+        frow = const.tile([P, 64], F32, name="frow")
+        nc.vector.memset(frow[:, 0:1], 1.0)
+        nc.vector.tensor_scalar_mul(out=frow[:, 0:1], in0=frow[:, 0:1], scalar1=1.0 / (2.0 * math.pi))
+        for step in range(6):
+            width = 2**step
+            nc.vector.tensor_scalar_mul(
+                out=frow[:, width : 2 * width], in0=frow[:, 0:width], scalar1=ratio**width
+            )
+        f2 = const.tile([P, 2, D], F32, name="f2")
+        frow_v = frow[:].rearrange("p (i e) -> p i e", e=2)
+        for h in range(2):
+            nc.vector.tensor_copy(out=f2[:, 0, 64 * h : 64 * h + 64], in_=frow[:])
+            fs_v = f2[:, 1, 64 * h : 64 * h + 64].rearrange("p (i e) -> p i e", e=2)
+            nc.vector.tensor_copy(out=fs_v[:, :, 0], in_=frow_v[:, :, 1])
+            nc.vector.tensor_scalar_mul(out=fs_v[:, :, 1], in0=frow_v[:, :, 0], scalar1=-1.0)
+        brow_f = const.tile([P, D], F32, name="brow_f")
+        nc.vector.tensor_copy(out=brow_f[:], in_=brow[:])
+
+        setup_ps = pso.tile([P, 4, P], F32, name="setup_ps", tag="o")
+        nc.tensor.transpose(setup_ps[:, 0, :], f2[:, 0, :], ident[:])
+        nc.tensor.transpose(setup_ps[:, 1, :], f2[:, 1, :], ident[:])
+        nc.tensor.transpose(setup_ps[:, 2, :], brow_f[:], ident[:])
+        cst = const.tile([P, 4], F32, name="cst")
+        nc.vector.tensor_copy(out=cst[:, 0:2], in_=setup_ps[:, 0:2, 0])
+        nc.vector.tensor_copy(out=cst[:, 2:4], in_=setup_ps[:, 2, 0:2])
+
+        wt_ps = psx.tile([P, 4, P], F32, name="wt_ps", tag="xt")
+        for w in range(2):
+            ww = w_sb[w][:].bitcast(F32)
+            for u in range(2):
+                nc.tensor.transpose(wt_ps[:, 2 * w + u, :], ww[:, P * u : P * u + P], ident[:])
+        wg = const.tile([P, 2 * D * 4], BF16, name="wg", align_bytes=64)
+        nc.vector.tensor_copy(
+            out=wg[:].bitcast(F32).rearrange("p (w d u) -> p w d u", w=2, u=2),
+            in_=wt_ps[:].rearrange("p (w u) d -> p w d u", u=2),
+        )
+        wc = const.tile([P, 2 * D], U32, name="wc", align_bytes=64)
+        ws = const.tile([P, 2 * D], U8, name="ws", align_bytes=64)
+        nc.vector.quantize_mx(out=wc[:].bitcast(FP8X4), scales=ws[:], in_=wg[:])
+
+        tf = const.tile([P, T], F32, name="tf")
+        nc.vector.tensor_copy(out=tf[:], in_=ti[:])
+        turns = const.tile([P, 2, T], F32, name="turns")
+        whole_i = const.tile([P, 2, T], I32, name="whole_i")
+        whole_f = const.tile([P, 2, T], F32, name="whole_f")
+        frac = const.tile([P, 2, T], F32, name="frac")
+        tab = const.tile([P, 2, T], F32, name="tab")
+        for j in range(2):
+            if j == 0:
+                nc.vector.tensor_scalar(
+                    out=turns[:, j, :], in0=tf[:], scalar1=cst[:, 0:1], scalar2=0.25,
+                    op0=ALU.mult, op1=ALU.add,
+                )
+            else:
+                nc.vector.tensor_scalar_mul(out=turns[:, j, :], in0=tf[:], scalar1=cst[:, 1:2])
+            nc.vector.tensor_copy(out=whole_i[:, j, :], in_=turns[:, j, :])
+            nc.vector.tensor_copy(out=whole_f[:, j, :], in_=whole_i[:, j, :])
+            nc.vector.tensor_tensor(
+                out=frac[:, j, :], in0=turns[:, j, :], in1=whole_f[:, j, :], op=ALU.subtract
+            )
+            nc.scalar.activation(out=tab[:, j, :], in_=frac[:, j, :], func=ACT.Sin, scale=2.0 * math.pi)
+
+        xg = {}
+        xq = {}
+        pp = {}
+        ab = {}
+
+        def xpose(n):
+            g = grp.tile([P, TI * K], BF16, name="xg", align_bytes=64)
+            gw = g[:].bitcast(F32)
+            xw = x_sb[n][:].bitcast(F32)
+            for h in range(2):
+                xt = psx.tile([P, 2, 2, P], F32, name="xt", tag="xt")
+                for i2 in range(2):
+                    for u in range(2):
+                        c0 = (2 * h + i2) * 256 + u * P
+                        nc.tensor.transpose(xt[:, i2, u, :], xw[:, c0 : c0 + P], ident[:])
+                nc.scalar.copy(
+                    out=gw[:, 512 * h : 512 * h + 512].rearrange("p (i t u) -> p i t u", i=2, u=2),
+                    in_=xt[:].rearrange("p i u t -> p i t u"),
+                )
+            xg[n] = g
+
+        def quant(n):
+            c = cod.tile([P, T], U32, name="xc", align_bytes=64)
+            s = cod.tile([P, T], U8, name="xs", align_bytes=64)
+            nc.vector.quantize_mx(out=c[:].bitcast(FP8X4), scales=s[:], in_=xg[n][:])
+            xq[n] = (c, s)
+
+        def mx(n):
+            c, s = xq[n]
+            for w in range(2):
+                acc = psp.tile([P, T], F32, name="acc")
+                nc.tensor.matmul_mx(
+                    out=acc[:],
+                    lhsT=wc[:, D * w : D * w + D].bitcast(FP8X4),
+                    lhsT_scale=ws[:, D * w : D * w + D],
+                    rhs=c[:].bitcast(FP8X4),
+                    rhs_scale=s[:],
+                    start=True,
+                    stop=True,
+                )
+                pp[(n, w)] = acc
+
+        def rope(n):
+            for w in range(2):
+                for j in range(2):
+                    t = prod.tile([P, T], F32, name="prod%d" % j)
+                    nc.vector.scalar_tensor_tensor(
+                        out=t[:], in0=pp[(n, w)][:], scalar=cst[:, 2 + w : 3 + w], in1=tab[:, j, :],
+                        op0=ALU.add, op1=ALU.mult,
+                    )
+                    ab[(n, w, j)] = t
+
+        def opose(n):
+            o_sb = ost.tile([P, 2, TI * D], F32, name="o_sb")
+            for w in range(2):
+                o = pso.tile([P, TI, D], F32, name="o", tag="o")
+                for i in range(TI):
+                    nc.tensor.matmul(
+                        o[:, i, :], lhsT=ab[(n, w, 0)][:, P * i : P * i + P], rhs=ident[:],
+                        is_transpose=True, start=True, stop=False,
+                    )
+                    nc.tensor.matmul(
+                        o[:, i, :], lhsT=ab[(n, w, 1)][:, P * i : P * i + P], rhs=perm[:],
+                        is_transpose=True, start=False, stop=True,
+                    )
+                nc.scalar.copy(out=o_sb[:, w, :], in_=o[:].rearrange("p i d -> p (i d)"))
+                nc.sync.dma_start(
+                    out=outs[w][n, 0].rearrange("(p i) d -> p (i d)", i=TI), in_=o_sb[:, w, :]
+                )
+
+        xpose(0)
+        quant(0)
+        mx(0)
+        xpose(1)
+        for k in range(NB + 1):
+            if k + 2 < NB:
+                xpose(k + 2)
+            if k + 1 < NB:
+                quant(k + 1)
+                mx(k + 1)
+            if k < NB:
+                rope(k)
+            if k >= 1:
+                opose(k - 1)

@@ -19,6 +19,7 @@ T = 512
 K = 512
 D = 128
 TI = 4
+GSET = ()
 
 FLOPS = 2 * NB * T * K * 2 * D
 
@@ -32,10 +33,12 @@ def tile_l1regressionmoeactionhead_pa_t_kernel(tc, x, W_qa, b_qa, W_qt, b_qt, ou
         grp = ctx.enter_context(tc.tile_pool(name="grp", bufs=3))
         cod = ctx.enter_context(tc.tile_pool(name="cod", bufs=3))
         prod = ctx.enter_context(tc.tile_pool(name="prod", bufs=4))
+        qsb = ctx.enter_context(tc.tile_pool(name="qsb", bufs=2)) if GSET else None
         ost = ctx.enter_context(tc.tile_pool(name="ost", bufs=4))
         psx = ctx.enter_context(tc.psum_pool(name="psx", bufs=2))
         psp = ctx.enter_context(tc.psum_pool(name="psp", bufs=4))
         pso = ctx.enter_context(tc.psum_pool(name="pso", bufs=2))
+        ctx.enter_context(tc.manual_schedule())
 
         w_sb = []
         for w, W in enumerate((W_qa, W_qt)):
@@ -43,7 +46,7 @@ def tile_l1regressionmoeactionhead_pa_t_kernel(tc, x, W_qa, b_qa, W_qt, b_qt, ou
             nc.scalar.dma_start(out=wt[:], in_=W)
             w_sb.append(wt)
         brow = const.tile([P, D], BF16, name="brow")
-        nc.vector.memset(brow[:], 0.0)
+        nc.gpsimd.memset(brow[:], 0.0)
         nc.scalar.dma_start(out=brow[0:1, :], in_=b_qa.unsqueeze(0))
         nc.scalar.dma_start(out=brow[1:2, :], in_=b_qt.unsqueeze(0))
         x_sb = []
@@ -52,43 +55,45 @@ def tile_l1regressionmoeactionhead_pa_t_kernel(tc, x, W_qa, b_qa, W_qt, b_qt, ou
             nc.sync.dma_start(out=xt_in[:], in_=x[n].rearrange("(p i) k -> p (i k)", i=TI))
             x_sb.append(xt_in)
 
+        tp = const.tile([P, P], I32, name="tp")
+        nc.gpsimd.iota(tp[:], pattern=[[TI, P]], base=0, channel_multiplier=0)
         ident = const.tile([P, P], F32, name="ident")
         make_identity(nc, ident[:])
-        perm = const.tile([P, P], F32, name="perm")
-        ident_v = ident[:].rearrange("p (i e) -> p i e", e=2)
-        perm_v = perm[:].rearrange("p (i e) -> p i e", e=2)
-        nc.vector.tensor_copy(out=perm_v[:, :, 0], in_=ident_v[:, :, 1])
-        nc.vector.tensor_copy(out=perm_v[:, :, 1], in_=ident_v[:, :, 0])
-
-        ti = const.tile([P, T], I32, name="ti")
-        nc.gpsimd.iota(ti[:], pattern=[[1, TI], [TI, P]], base=0, channel_multiplier=0)
 
         ratio = 10000.0 ** (-1.0 / 64.0)
-        frow = const.tile([P, 64], F32, name="frow")
-        nc.vector.memset(frow[:, 0:1], 1.0)
-        nc.vector.tensor_scalar_mul(out=frow[:, 0:1], in0=frow[:, 0:1], scalar1=1.0 / (2.0 * math.pi))
-        for step in range(6):
+        f2 = const.tile([P, 2, D], F32, name="f2")
+        nc.vector.memset(f2[:, 0, 0:1], 1.0)
+        nc.vector.tensor_scalar_mul(out=f2[:, 0, 0:1], in0=f2[:, 0, 0:1], scalar1=1.0 / (2.0 * math.pi))
+        junk = const.tile([P, 1], F32, name="junk")
+        nc.scalar.activation(out=junk[:], in_=f2[:, 0, 0:1], func=ACT.Sin)
+        for step in range(7):
             width = 2**step
             nc.vector.tensor_scalar_mul(
-                out=frow[:, width : 2 * width], in0=frow[:, 0:width], scalar1=ratio**width
+                out=f2[:, 0, width : 2 * width], in0=f2[:, 0, 0:width],
+                scalar1=(ratio**width if step < 6 else 1.0),
             )
-        f2 = const.tile([P, 2, D], F32, name="f2")
-        frow_v = frow[:].rearrange("p (i e) -> p i e", e=2)
-        for h in range(2):
-            nc.vector.tensor_copy(out=f2[:, 0, 64 * h : 64 * h + 64], in_=frow[:])
-            fs_v = f2[:, 1, 64 * h : 64 * h + 64].rearrange("p (i e) -> p i e", e=2)
-            nc.vector.tensor_copy(out=fs_v[:, :, 0], in_=frow_v[:, :, 1])
-            nc.vector.tensor_scalar_mul(out=fs_v[:, :, 1], in0=frow_v[:, :, 0], scalar1=-1.0)
-        brow_f = const.tile([P, D], F32, name="brow_f")
-        nc.vector.tensor_copy(out=brow_f[:], in_=brow[:])
+        fc_v = f2[:, 0, :].rearrange("p (i e) -> p i e", e=2)
+        fs_v = f2[:, 1, :].rearrange("p (i e) -> p i e", e=2)
+        nc.vector.tensor_copy(out=fs_v[:, :, 0], in_=fc_v[:, :, 1])
+        nc.vector.tensor_scalar_mul(out=fs_v[:, :, 1], in0=fc_v[:, :, 0], scalar1=-1.0)
+        setup_f = pso.tile([P, 2, P], F32, name="setup_f", tag="o")
+        nc.tensor.transpose(setup_f[:, 0, :], f2[:, 0, :], ident[:])
+        nc.tensor.transpose(setup_f[:, 1, :], f2[:, 1, :], ident[:])
+        tf = const.tile([P, T], F32, name="tf")
+        for i in range(TI):
+            nc.vector.tensor_scalar_add(out=tf[:, P * i : P * i + P], in0=tp[:], scalar1=float(i))
+        cstf = const.tile([P, 2], F32, name="cstf")
+        nc.vector.tensor_copy(out=cstf[:], in_=setup_f[:, :, 0])
 
-        setup_ps = pso.tile([P, 4, P], F32, name="setup_ps", tag="o")
-        nc.tensor.transpose(setup_ps[:, 0, :], f2[:, 0, :], ident[:])
-        nc.tensor.transpose(setup_ps[:, 1, :], f2[:, 1, :], ident[:])
-        nc.tensor.transpose(setup_ps[:, 2, :], brow_f[:], ident[:])
-        cst = const.tile([P, 4], F32, name="cst")
-        nc.vector.tensor_copy(out=cst[:, 0:2], in_=setup_ps[:, 0:2, 0])
-        nc.vector.tensor_copy(out=cst[:, 2:4], in_=setup_ps[:, 2, 0:2])
+        turns = const.tile([P, T], F32, name="turns")
+        whole = const.tile([P, 2, T], I32, name="whole")
+        frac = const.tile([P, 2, T], F32, name="frac")
+        tab = const.tile([P, 2, T], F32, name="tab")
+        nc.vector.tensor_scalar(
+            out=turns[:], in0=tf[:], scalar1=cstf[:, 0:1], scalar2=0.25, op0=ALU.mult, op1=ALU.add
+        )
+        nc.vector.tensor_copy(out=whole[:, 0, :], in_=turns[:])
+        nc.vector.tensor_tensor(out=frac[:, 0, :], in0=turns[:], in1=whole[:, 0, :], op=ALU.subtract)
 
         wt_ps = psx.tile([P, 4, P], F32, name="wt_ps", tag="xt")
         for w in range(2):
@@ -96,42 +101,18 @@ def tile_l1regressionmoeactionhead_pa_t_kernel(tc, x, W_qa, b_qa, W_qt, b_qt, ou
             for u in range(2):
                 nc.tensor.transpose(wt_ps[:, 2 * w + u, :], ww[:, P * u : P * u + P], ident[:])
         wg = const.tile([P, 2 * D * 4], BF16, name="wg", align_bytes=64)
-        nc.vector.tensor_copy(
+        nc.scalar.copy(
             out=wg[:].bitcast(F32).rearrange("p (w d u) -> p w d u", w=2, u=2),
             in_=wt_ps[:].rearrange("p (w u) d -> p w d u", u=2),
         )
-        wc = const.tile([P, 2 * D], U32, name="wc", align_bytes=64)
-        ws = const.tile([P, 2 * D], U8, name="ws", align_bytes=64)
-        nc.vector.quantize_mx(out=wc[:].bitcast(FP8X4), scales=ws[:], in_=wg[:])
-
-        tf = const.tile([P, T], F32, name="tf")
-        nc.vector.tensor_copy(out=tf[:], in_=ti[:])
-        turns = const.tile([P, 2, T], F32, name="turns")
-        whole_i = const.tile([P, 2, T], I32, name="whole_i")
-        whole_f = const.tile([P, 2, T], F32, name="whole_f")
-        frac = const.tile([P, 2, T], F32, name="frac")
-        tab = const.tile([P, 2, T], F32, name="tab")
-        for j in range(2):
-            if j == 0:
-                nc.vector.tensor_scalar(
-                    out=turns[:, j, :], in0=tf[:], scalar1=cst[:, 0:1], scalar2=0.25,
-                    op0=ALU.mult, op1=ALU.add,
-                )
-            else:
-                nc.vector.tensor_scalar_mul(out=turns[:, j, :], in0=tf[:], scalar1=cst[:, 1:2])
-            nc.vector.tensor_copy(out=whole_i[:, j, :], in_=turns[:, j, :])
-            nc.vector.tensor_copy(out=whole_f[:, j, :], in_=whole_i[:, j, :])
-            nc.vector.tensor_tensor(
-                out=frac[:, j, :], in0=turns[:, j, :], in1=whole_f[:, j, :], op=ALU.subtract
-            )
-            nc.scalar.activation(out=tab[:, j, :], in_=frac[:, j, :], func=ACT.Sin, scale=2.0 * math.pi)
 
         xg = {}
         xq = {}
         pp = {}
         ab = {}
+        osb = {}
 
-        def xpose(n):
+        def xpose(n, second_on_vector=False):
             g = grp.tile([P, TI * K], BF16, name="xg", align_bytes=64)
             gw = g[:].bitcast(F32)
             xw = x_sb[n][:].bitcast(F32)
@@ -141,10 +122,12 @@ def tile_l1regressionmoeactionhead_pa_t_kernel(tc, x, W_qa, b_qa, W_qt, b_qt, ou
                     for u in range(2):
                         c0 = (2 * h + i2) * 256 + u * P
                         nc.tensor.transpose(xt[:, i2, u, :], xw[:, c0 : c0 + P], ident[:])
-                nc.scalar.copy(
-                    out=gw[:, 512 * h : 512 * h + 512].rearrange("p (i t u) -> p i t u", i=2, u=2),
-                    in_=xt[:].rearrange("p i u t -> p i t u"),
-                )
+                dst = gw[:, 512 * h : 512 * h + 512].rearrange("p (i t u) -> p i t u", i=2, u=2)
+                src = xt[:].rearrange("p i u t -> p i t u")
+                if h == 1 and second_on_vector:
+                    nc.vector.tensor_copy(out=dst, in_=src)
+                else:
+                    nc.scalar.copy(out=dst, in_=src)
             xg[n] = g
 
         def quant(n):
@@ -169,44 +152,77 @@ def tile_l1regressionmoeactionhead_pa_t_kernel(tc, x, W_qa, b_qa, W_qt, b_qt, ou
                 pp[(n, w)] = acc
 
         def rope(n):
-            for w in range(2):
+            if n in GSET:
+                q = qsb.tile([P, T], F32, name="q")
+                nc.scalar.activation(out=q[:], in_=pp[(n, 1)][:], func=ACT.Identity, bias=cstb[:, 1:2])
+                for j in range(2):
+                    t = prod.tile([P, T], F32, name="prod%d" % j)
+                    nc.gpsimd.tensor_tensor(out=t[:], in0=q[:], in1=tab[:, j, :], op=ALU.mult)
+                    ab[(n, 1, j)] = t
+            for w in range(1 if n in GSET else 2):
                 for j in range(2):
                     t = prod.tile([P, T], F32, name="prod%d" % j)
                     nc.vector.scalar_tensor_tensor(
-                        out=t[:], in0=pp[(n, w)][:], scalar=cst[:, 2 + w : 3 + w], in1=tab[:, j, :],
+                        out=t[:], in0=pp[(n, w)][:], scalar=cstb[:, w : w + 1], in1=tab[:, j, :],
                         op0=ALU.add, op1=ALU.mult,
                     )
                     ab[(n, w, j)] = t
 
-        def opose(n):
-            o_sb = ost.tile([P, 2, TI * D], F32, name="o_sb")
-            for w in range(2):
-                o = pso.tile([P, TI, D], F32, name="o", tag="o")
-                for i in range(TI):
-                    nc.tensor.matmul(
-                        o[:, i, :], lhsT=ab[(n, w, 0)][:, P * i : P * i + P], rhs=ident[:],
-                        is_transpose=True, start=True, stop=False,
-                    )
-                    nc.tensor.matmul(
-                        o[:, i, :], lhsT=ab[(n, w, 1)][:, P * i : P * i + P], rhs=perm[:],
-                        is_transpose=True, start=False, stop=True,
-                    )
-                nc.scalar.copy(out=o_sb[:, w, :], in_=o[:].rearrange("p i d -> p (i d)"))
-                nc.sync.dma_start(
-                    out=outs[w][n, 0].rearrange("(p i) d -> p (i d)", i=TI), in_=o_sb[:, w, :]
+        def opose(n, w):
+            if w == 0:
+                osb[n] = ost.tile([P, 2, TI * D], F32, name="o_sb")
+            o_sb = osb[n]
+            o = pso.tile([P, TI, D], F32, name="o", tag="o")
+            for i in range(TI):
+                nc.tensor.matmul(
+                    o[:, i, :], lhsT=ab[(n, w, 0)][:, P * i : P * i + P], rhs=ident[:],
+                    is_transpose=True, start=True, stop=False,
                 )
+                nc.tensor.matmul(
+                    o[:, i, :], lhsT=ab[(n, w, 1)][:, P * i : P * i + P], rhs=perm[:],
+                    is_transpose=True, start=False, stop=True,
+                )
+            nc.scalar.copy(out=o_sb[:, w, :], in_=o[:].rearrange("p i d -> p (i d)"))
+            nc.sync.dma_start(out=outs[w][n, 0].rearrange("(p i) d -> p (i d)", i=TI), in_=o_sb[:, w, :])
 
         xpose(0)
+        perm = const.tile([P, P], F32, name="perm")
+        ident_v = ident[:].rearrange("p (i e) -> p i e", e=2)
+        perm_v = perm[:].rearrange("p (i e) -> p i e", e=2)
+        nc.gpsimd.tensor_copy(out=perm_v[:, :, 0], in_=ident_v[:, :, 1])
+        nc.gpsimd.tensor_copy(out=perm_v[:, :, 1], in_=ident_v[:, :, 0])
+        brow_f = const.tile([P, D], F32, name="brow_f")
+        nc.gpsimd.tensor_copy(out=brow_f[:], in_=brow[:])
+        nc.vector.tensor_scalar_mul(out=whole[:, 1, :], in0=tf[:], scalar1=cstf[:, 1:2])
+        nc.vector.scalar_tensor_tensor(
+            out=frac[:, 1, :], in0=tf[:], scalar=cstf[:, 1:2], in1=whole[:, 1, :],
+            op0=ALU.mult, op1=ALU.subtract,
+        )
+        wc = const.tile([P, 2 * D], U32, name="wc", align_bytes=64)
+        ws = const.tile([P, 2 * D], U8, name="ws", align_bytes=64)
+        nc.vector.quantize_mx(out=wc[:].bitcast(FP8X4), scales=ws[:], in_=wg[:])
         quant(0)
+        xpose(1, second_on_vector=True)
+        setup_b = pso.tile([P, P], F32, name="setup_b", tag="o")
+        nc.tensor.transpose(setup_b[:], brow_f[:], ident[:])
+        nc.scalar.activation(out=tab[:, 0, :], in_=frac[:, 0, :], func=ACT.Sin, scale=2.0 * math.pi)
+        nc.scalar.activation(out=tab[:, 1, :], in_=frac[:, 1, :], func=ACT.Sin, scale=2.0 * math.pi)
         mx(0)
-        xpose(1)
+        cstb = const.tile([P, 2], F32, name="cstb")
+        nc.vector.tensor_copy(out=cstb[:], in_=setup_b[:, 0:2])
+        quant(1)
+        xpose(2)
+
         for k in range(NB + 1):
-            if k + 2 < NB:
-                xpose(k + 2)
             if k + 1 < NB:
-                quant(k + 1)
                 mx(k + 1)
             if k < NB:
                 rope(k)
             if k >= 1:
-                opose(k - 1)
+                opose(k - 1, 0)
+            if k + 3 < NB:
+                xpose(k + 3)
+            if k >= 1:
+                opose(k - 1, 1)
+            if k + 2 < NB:
+                quant(k + 2)

@@ -19,7 +19,7 @@ T = 512
 K = 512
 D = 128
 TI = 4
-GSET = ()
+GSET = (0, 2, 4, 6, 8, 10, 12, 14)
 
 FLOPS = 2 * NB * T * K * 2 * D
 

@@ -19,7 +19,7 @@ T = 512
 K = 512
 D = 128
 TI = 4
-GSET = (0, 2, 4, 6, 8, 10, 12, 14)
+GSET = ()
 
 FLOPS = 2 * NB * T * K * 2 * D
 
@@ -110,7 +110,6 @@ def tile_l1regressionmoeactionhead_pa_t_kernel(tc, x, W_qa, b_qa, W_qt, b_qt, ou
         xq = {}
         pp = {}
         ab = {}
-        osb = {}
 
         def xpose(n, second_on_vector=False):
             g = grp.tile([P, TI * K], BF16, name="xg", align_bytes=64)
@@ -168,22 +167,24 @@ def tile_l1regressionmoeactionhead_pa_t_kernel(tc, x, W_qa, b_qa, W_qt, b_qt, ou
                     )
                     ab[(n, w, j)] = t
 
-        def opose(n, w):
-            if w == 0:
-                osb[n] = ost.tile([P, 2, TI * D], F32, name="o_sb")
-            o_sb = osb[n]
-            o = pso.tile([P, TI, D], F32, name="o", tag="o")
-            for i in range(TI):
+        def opose(n):
+            o_sb = ost.tile([P, 2, TI * D], F32, name="o_sb")
+            o = []
+            for w in range(2):
+                o.append(pso.tile([P, TI, D], F32, name="o%d" % w, tag="o"))
+            if n < NB - 1:
+                steps = [(i, j, w) for i in range(TI) for j in range(2) for w in range(2)]
+            else:
+                steps = [(i, j, w) for w in range(2) for i in range(TI) for j in range(2)]
+            for i, j, w in steps:
                 nc.tensor.matmul(
-                    o[:, i, :], lhsT=ab[(n, w, 0)][:, P * i : P * i + P], rhs=ident[:],
-                    is_transpose=True, start=True, stop=False,
+                    o[w][:, i, :], lhsT=ab[(n, w, j)][:, P * i : P * i + P],
+                    rhs=(ident[:] if j == 0 else perm[:]),
+                    is_transpose=True, start=(j == 0), stop=(j == 1),
                 )
-                nc.tensor.matmul(
-                    o[:, i, :], lhsT=ab[(n, w, 1)][:, P * i : P * i + P], rhs=perm[:],
-                    is_transpose=True, start=False, stop=True,
-                )
-            nc.scalar.copy(out=o_sb[:, w, :], in_=o[:].rearrange("p i d -> p (i d)"))
-            nc.sync.dma_start(out=outs[w][n, 0].rearrange("(p i) d -> p (i d)", i=TI), in_=o_sb[:, w, :])
+            for w in range(2):
+                nc.scalar.copy(out=o_sb[:, w, :], in_=o[w][:].rearrange("p i d -> p (i d)"))
+                nc.sync.dma_start(out=outs[w][n, 0].rearrange("(p i) d -> p (i d)", i=TI), in_=o_sb[:, w, :])
 
         xpose(0)
         perm = const.tile([P, P], F32, name="perm")
@@ -219,10 +220,8 @@ def tile_l1regressionmoeactionhead_pa_t_kernel(tc, x, W_qa, b_qa, W_qt, b_qt, ou
             if k < NB:
                 rope(k)
             if k >= 1:
-                opose(k - 1, 0)
+                opose(k - 1)
             if k + 3 < NB:
                 xpose(k + 3)
-            if k >= 1:
-                opose(k - 1, 1)
             if k + 2 < NB:
                 quant(k + 2)

@@ -52,7 +52,12 @@ def tile_l1regressionmoeactionhead_pa_t_kernel(tc, x, W_qa, b_qa, W_qt, b_qt, ou
         x_sb = []
         for n in range(NB):
             xt_in = xin.tile([P, TI * K], BF16, name="x_sb")
-            nc.sync.dma_start(out=xt_in[:], in_=x[n].rearrange("(p i) k -> p (i k)", i=TI))
+            src_n = x[n].rearrange("(p i) k -> p (i k)", i=TI)
+            if n == 0:
+                nc.sync.dma_start(out=xt_in[:, 0 : 2 * K], in_=src_n[:, 0 : 2 * K])
+                nc.sync.dma_start(out=xt_in[:, 2 * K : 4 * K], in_=src_n[:, 2 * K : 4 * K])
+            else:
+                nc.sync.dma_start(out=xt_in[:], in_=src_n)
             x_sb.append(xt_in)
 
         tp = const.tile([P, P], I32, name="tp")
@@ -110,6 +115,7 @@ def tile_l1regressionmoeactionhead_pa_t_kernel(tc, x, W_qa, b_qa, W_qt, b_qt, ou
         xq = {}
         pp = {}
         ab = {}
+        osb = {}
 
         def xpose(n, second_on_vector=False):
             g = grp.tile([P, TI * K], BF16, name="xg", align_bytes=64)
@@ -159,32 +165,40 @@ def tile_l1regressionmoeactionhead_pa_t_kernel(tc, x, W_qa, b_qa, W_qt, b_qt, ou
                     nc.gpsimd.tensor_tensor(out=t[:], in0=q[:], in1=tab[:, j, :], op=ALU.mult)
                     ab[(n, 1, j)] = t
             for w in range(1 if n in GSET else 2):
+                pieces = 2 if (n == NB - 1 and w == 1) else 1
                 for j in range(2):
-                    t = prod.tile([P, T], F32, name="prod%d" % j)
-                    nc.vector.scalar_tensor_tensor(
-                        out=t[:], in0=pp[(n, w)][:], scalar=cstb[:, w : w + 1], in1=tab[:, j, :],
-                        op0=ALU.add, op1=ALU.mult,
-                    )
-                    ab[(n, w, j)] = t
+                    ab[(n, w, j)] = prod.tile([P, T], F32, name="prod%d" % j)
+                size = T // pieces
+                for piece in range(pieces):
+                    cols = slice(piece * size, piece * size + size)
+                    for j in range(2):
+                        nc.vector.scalar_tensor_tensor(
+                            out=ab[(n, w, j)][:, cols], in0=pp[(n, w)][:, cols], scalar=cstb[:, w : w + 1],
+                            in1=tab[:, j, cols], op0=ALU.add, op1=ALU.mult,
+                        )
 
-        def opose(n):
-            o_sb = ost.tile([P, 2, TI * D], F32, name="o_sb")
-            o = []
-            for w in range(2):
-                o.append(pso.tile([P, TI, D], F32, name="o%d" % w, tag="o"))
-            if n < NB - 1:
-                steps = [(i, j, w) for i in range(TI) for j in range(2) for w in range(2)]
-            else:
-                steps = [(i, j, w) for w in range(2) for i in range(TI) for j in range(2)]
-            for i, j, w in steps:
-                nc.tensor.matmul(
-                    o[w][:, i, :], lhsT=ab[(n, w, j)][:, P * i : P * i + P],
-                    rhs=(ident[:] if j == 0 else perm[:]),
-                    is_transpose=True, start=(j == 0), stop=(j == 1),
-                )
-            for w in range(2):
-                nc.scalar.copy(out=o_sb[:, w, :], in_=o[w][:].rearrange("p i d -> p (i d)"))
-                nc.sync.dma_start(out=outs[w][n, 0].rearrange("(p i) d -> p (i d)", i=TI), in_=o_sb[:, w, :])
+        def opose(n, w):
+            if w == 0:
+                osb[n] = ost.tile([P, 2, TI * D], F32, name="o_sb")
+            o_sb = osb[n]
+            dst = outs[w][n, 0].rearrange("(p i) d -> p (i d)", i=TI)
+            pieces = 2 if (n == NB - 1 and w == 1) else 1
+            tiles = TI // pieces
+            for piece in range(pieces):
+                o = pso.tile([P, tiles, D], F32, name="o", tag="o")
+                for i2 in range(tiles):
+                    i = piece * tiles + i2
+                    nc.tensor.matmul(
+                        o[:, i2, :], lhsT=ab[(n, w, 0)][:, P * i : P * i + P], rhs=ident[:],
+                        is_transpose=True, start=True, stop=False,
+                    )
+                    nc.tensor.matmul(
+                        o[:, i2, :], lhsT=ab[(n, w, 1)][:, P * i : P * i + P], rhs=perm[:],
+                        is_transpose=True, start=False, stop=True,
+                    )
+                cols = slice(piece * tiles * D, (piece + 1) * tiles * D)
+                nc.scalar.copy(out=o_sb[:, w, cols], in_=o[:].rearrange("p i d -> p (i d)"))
+                nc.sync.dma_start(out=dst[:, cols], in_=o_sb[:, w, cols])
 
         xpose(0)
         perm = const.tile([P, P], F32, name="perm")
@@ -220,8 +234,10 @@ def tile_l1regressionmoeactionhead_pa_t_kernel(tc, x, W_qa, b_qa, W_qt, b_qt, ou
             if k < NB:
                 rope(k)
             if k >= 1:
-                opose(k - 1)
+                opose(k - 1, 0)
             if k + 3 < NB:
                 xpose(k + 3)
+            if k >= 1:
+                opose(k - 1, 1)
             if k + 2 < NB:
                 quant(k + 2)

import math
from contextlib import ExitStack

import concourse.mybir as mybir
from concourse.masks import make_identity

F32 = mybir.dt.float32
BF16 = mybir.dt.bfloat16
I32 = mybir.dt.int32
U32 = mybir.dt.uint32
U8 = mybir.dt.uint8
FP8X4 = mybir.dt.float8_e4m3fn_x4
ALU = mybir.AluOpType
ACT = mybir.ActivationFunctionType

P = 128
NB = 16
T = 512
K = 512
D = 128
TI = 4
GSET = ()

FLOPS = 2 * NB * T * K * 2 * D


def tile_l1regressionmoeactionhead_pa_t_kernel(tc, x, W_qa, b_qa, W_qt, b_qt, out_0, out_1):
    nc = tc.nc
    outs = (out_0, out_1)
    with ExitStack() as ctx:
        const = ctx.enter_context(tc.tile_pool(name="const", bufs=1))
        xin = ctx.enter_context(tc.tile_pool(name="xin", bufs=NB))
        grp = ctx.enter_context(tc.tile_pool(name="grp", bufs=3))
        cod = ctx.enter_context(tc.tile_pool(name="cod", bufs=3))
        prod = ctx.enter_context(tc.tile_pool(name="prod", bufs=4))
        qsb = ctx.enter_context(tc.tile_pool(name="qsb", bufs=2)) if GSET else None
        ost = ctx.enter_context(tc.tile_pool(name="ost", bufs=4))
        psx = ctx.enter_context(tc.psum_pool(name="psx", bufs=2))
        psp = ctx.enter_context(tc.psum_pool(name="psp", bufs=4))
        pso = ctx.enter_context(tc.psum_pool(name="pso", bufs=2))
        ctx.enter_context(tc.manual_schedule())

        w_sb = []
        for w, W in enumerate((W_qa, W_qt)):
            wt = const.tile([P, K], BF16, name="w_sb%d" % w)
            nc.scalar.dma_start(out=wt[:], in_=W)
            w_sb.append(wt)
        brow = const.tile([P, D], BF16, name="brow")
        nc.gpsimd.memset(brow[:], 0.0)
        nc.scalar.dma_start(out=brow[0:1, :], in_=b_qa.unsqueeze(0))
        nc.scalar.dma_start(out=brow[1:2, :], in_=b_qt.unsqueeze(0))
        x_sb = []
        for n in range(NB):
            xt_in = xin.tile([P, TI * K], BF16, name="x_sb")
            src_n = x[n].rearrange("(p i) k -> p (i k)", i=TI)
            if n == 0:
                nc.sync.dma_start(out=xt_in[:, 0 : 2 * K], in_=src_n[:, 0 : 2 * K])
                nc.sync.dma_start(out=xt_in[:, 2 * K : 4 * K], in_=src_n[:, 2 * K : 4 * K])
            else:
                nc.sync.dma_start(out=xt_in[:], in_=src_n)
            x_sb.append(xt_in)

        tp = const.tile([P, P], I32, name="tp")
        nc.gpsimd.iota(tp[:], pattern=[[TI, P]], base=0, channel_multiplier=0)
        ident = const.tile([P, P], F32, name="ident")
        make_identity(nc, ident[:])

        ratio = 10000.0 ** (-1.0 / 64.0)
        f2 = const.tile([P, 2, D], F32, name="f2")
        nc.vector.memset(f2[:, 0, 0:1], 1.0)
        nc.vector.tensor_scalar_mul(out=f2[:, 0, 0:1], in0=f2[:, 0, 0:1], scalar1=1.0 / (2.0 * math.pi))
        junk = const.tile([P, 1], F32, name="junk")
        nc.scalar.activation(out=junk[:], in_=f2[:, 0, 0:1], func=ACT.Sin)
        for step in range(7):
            width = 2**step
            nc.vector.tensor_scalar_mul(
                out=f2[:, 0, width : 2 * width], in0=f2[:, 0, 0:width],
                scalar1=(ratio**width if step < 6 else 1.0),
            )
        fc_v = f2[:, 0, :].rearrange("p (i e) -> p i e", e=2)
        fs_v = f2[:, 1, :].rearrange("p (i e) -> p i e", e=2)
        nc.vector.tensor_copy(out=fs_v[:, :, 0], in_=fc_v[:, :, 1])
        nc.vector.tensor_scalar_mul(out=fs_v[:, :, 1], in0=fc_v[:, :, 0], scalar1=-1.0)
        setup_f = pso.tile([P, 2, P], F32, name="setup_f", tag="o")
        nc.tensor.transpose(setup_f[:, 0, :], f2[:, 0, :], ident[:])
        nc.tensor.transpose(setup_f[:, 1, :], f2[:, 1, :], ident[:])
        tf = const.tile([P, T], F32, name="tf")
        for i in range(TI):
            nc.vector.tensor_scalar_add(out=tf[:, P * i : P * i + P], in0=tp[:], scalar1=float(i))
        cstf = const.tile([P, 2], F32, name="cstf")
        nc.vector.tensor_copy(out=cstf[:], in_=setup_f[:, :, 0])

        turns = const.tile([P, T], F32, name="turns")
        whole = const.tile([P, 2, T], I32, name="whole")
        frac = const.tile([P, 2, T], F32, name="frac")
        tab = const.tile([P, 2, T], F32, name="tab")
        nc.vector.tensor_scalar(
            out=turns[:], in0=tf[:], scalar1=cstf[:, 0:1], scalar2=0.25, op0=ALU.mult, op1=ALU.add
        )
        nc.vector.tensor_copy(out=whole[:, 0, :], in_=turns[:])
        nc.vector.tensor_tensor(out=frac[:, 0, :], in0=turns[:], in1=whole[:, 0, :], op=ALU.subtract)

        wt_ps = psx.tile([P, 4, P], F32, name="wt_ps", tag="xt")
        for w in range(2):
            ww = w_sb[w][:].bitcast(F32)
            for u in range(2):
                nc.tensor.transpose(wt_ps[:, 2 * w + u, :], ww[:, P * u : P * u + P], ident[:])
        wg = const.tile([P, 2 * D * 4], BF16, name="wg", align_bytes=64)
        nc.scalar.copy(
            out=wg[:].bitcast(F32).rearrange("p (w d u) -> p w d u", w=2, u=2),
            in_=wt_ps[:].rearrange("p (w u) d -> p w d u", u=2),
        )

        xg = {}
        xq = {}
        pp = {}
        ab = {}
        osb = {}

        def xpose(n, second_on_vector=False):
            g = grp.tile([P, TI * K], BF16, name="xg", align_bytes=64)
            gw = g[:].bitcast(F32)
            xw = x_sb[n][:].bitcast(F32)
            for h in range(2):
                xt = psx.tile([P, 2, 2, P], F32, name="xt", tag="xt")
                for i2 in range(2):
                    for u in range(2):
                        c0 = (2 * h + i2) * 256 + u * P
                        nc.tensor.transpose(xt[:, i2, u, :], xw[:, c0 : c0 + P], ident[:])
                dst = gw[:, 512 * h : 512 * h + 512].rearrange("p (i t u) -> p i t u", i=2, u=2)
                src = xt[:].rearrange("p i u t -> p i t u")
                if h == 1 and second_on_vector:
                    nc.vector.tensor_copy(out=dst, in_=src)
                else:
                    nc.scalar.copy(out=dst, in_=src)
            xg[n] = g

        def quant(n):
            c = cod.tile([P, T], U32, name="xc", align_bytes=64)
            s = cod.tile([P, T], U8, name="xs", align_bytes=64)
            nc.vector.quantize_mx(out=c[:].bitcast(FP8X4), scales=s[:], in_=xg[n][:])
            xq[n] = (c, s)

        def mx(n):
            c, s = xq[n]
            for w in range(2):
                acc = psp.tile([P, T], F32, name="acc")
                nc.tensor.matmul_mx(
                    out=acc[:],
                    lhsT=wc[:, D * w : D * w + D].bitcast(FP8X4),
                    lhsT_scale=ws[:, D * w : D * w + D],
                    rhs=c[:].bitcast(FP8X4),
                    rhs_scale=s[:],
                    start=True,
                    stop=True,
                )
                pp[(n, w)] = acc

        def rope(n):
            if n in GSET:
                q = qsb.tile([P, T], F32, name="q")
                nc.scalar.activation(out=q[:], in_=pp[(n, 1)][:], func=ACT.Identity, bias=cstb[:, 1:2])
                for j in range(2):
                    t = prod.tile([P, T], F32, name="prod%d" % j)
                    nc.gpsimd.tensor_tensor(out=t[:], in0=q[:], in1=tab[:, j, :], op=ALU.mult)
                    ab[(n, 1, j)] = t
            for w in range(1 if n in GSET else 2):
                pieces = 2 if (n == NB - 1 and w == 1) else 1
                for j in range(2):
                    ab[(n, w, j)] = prod.tile([P, T], F32, name="prod%d" % j)
                size = T // pieces
                for piece in range(pieces):
                    cols = slice(piece * size, piece * size + size)
                    for j in range(2):
                        nc.vector.scalar_tensor_tensor(
                            out=ab[(n, w, j)][:, cols], in0=pp[(n, w)][:, cols], scalar=cstb[:, w : w + 1],
                            in1=tab[:, j, cols], op0=ALU.add, op1=ALU.mult,
                        )

        def opose(n, w):
            if w == 0:
                osb[n] = ost.tile([P, 2, TI * D], F32, name="o_sb")
            o_sb = osb[n]
            dst = outs[w][n, 0].rearrange("(p i) d -> p (i d)", i=TI)
            pieces = 2 if (n == NB - 1 and w == 1) else 1
            tiles = TI // pieces
            for piece in range(pieces):
                o = pso.tile([P, tiles, D], F32, name="o", tag="o")
                for i2 in range(tiles):
                    i = piece * tiles + i2
                    nc.tensor.matmul(
                        o[:, i2, :], lhsT=ab[(n, w, 0)][:, P * i : P * i + P], rhs=ident[:],
                        is_transpose=True, start=True, stop=False,
                    )
                    nc.tensor.matmul(
                        o[:, i2, :], lhsT=ab[(n, w, 1)][:, P * i : P * i + P], rhs=perm[:],
                        is_transpose=True, start=False, stop=True,
                    )
                cols = slice(piece * tiles * D, (piece + 1) * tiles * D)
                nc.scalar.copy(out=o_sb[:, w, cols], in_=o[:].rearrange("p i d -> p (i d)"))
                nc.sync.dma_start(out=dst[:, cols], in_=o_sb[:, w, cols])

        xpose(0)
        perm = const.tile([P, P], F32, name="perm")
        ident_v = ident[:].rearrange("p (i e) -> p i e", e=2)
        perm_v = perm[:].rearrange("p (i e) -> p i e", e=2)
        nc.gpsimd.tensor_copy(out=perm_v[:, :, 0], in_=ident_v[:, :, 1])
        nc.gpsimd.tensor_copy(out=perm_v[:, :, 1], in_=ident_v[:, :, 0])
        brow_f = const.tile([P, D], F32, name="brow_f")
        nc.gpsimd.tensor_copy(out=brow_f[:], in_=brow[:])
        nc.vector.tensor_scalar_mul(out=whole[:, 1, :], in0=tf[:], scalar1=cstf[:, 1:2])
        nc.vector.scalar_tensor_tensor(
            out=frac[:, 1, :], in0=tf[:], scalar=cstf[:, 1:2], in1=whole[:, 1, :],
            op0=ALU.mult, op1=ALU.subtract,
        )
        wc = const.tile([P, 2 * D], U32, name="wc", align_bytes=64)
        ws = const.tile([P, 2 * D], U8, name="ws", align_bytes=64)
        nc.vector.quantize_mx(out=wc[:].bitcast(FP8X4), scales=ws[:], in_=wg[:])
        quant(0)
        xpose(1, second_on_vector=True)
        setup_b = pso.tile([P, P], F32, name="setup_b", tag="o")
        nc.tensor.transpose(setup_b[:], brow_f[:], ident[:])
        nc.scalar.activation(out=tab[:, 0, :], in_=frac[:, 0, :], func=ACT.Sin, scale=2.0 * math.pi)
        nc.scalar.activation(out=tab[:, 1, :], in_=frac[:, 1, :], func=ACT.Sin, scale=2.0 * math.pi)
        mx(0)
        cstb = const.tile([P, 2], F32, name="cstb")
        nc.vector.tensor_copy(out=cstb[:], in_=setup_b[:, 0:2])
        quant(1)
        xpose(2)

        for k in range(NB + 1):
            if k + 1 < NB:
                mx(k + 1)
            if k < NB:
                rope(k)
            if k >= 1:
                opose(k - 1, 0)
            if k + 3 < NB:
                xpose(k + 3)
            if k >= 1:
                opose(k - 1, 1)
            if k + 2 < NB:
                quant(k + 2)
